import numpy as np
import ml_dtypes


def mxq(x, axis, fmt="e4m3"):
    dtype, down = {"e4m3": (ml_dtypes.float8_e4m3fn, 7), "e5m2": (ml_dtypes.float8_e5m2, 14)}[fmt]
    v = np.moveaxis(np.asarray(x, np.float32).astype(ml_dtypes.bfloat16).astype(np.float64), axis, -1)
    blocks = v.reshape(v.shape[:-1] + (-1, 32))
    amax = np.abs(blocks).max(-1, keepdims=True)
    byte = np.maximum(np.where(amax > 0, np.frexp(amax)[1] - 1 + 127, 0) - down, 1)
    scale = np.exp2(byte - 127.0)
    codes = (blocks / scale).astype(np.float32).astype(dtype).astype(np.float64)
    return np.moveaxis((codes * scale).reshape(v.shape), -1, axis)


WIDE = False


def mx_kscale(k):
    if not WIDE:
        return np.ones(k)
    levels = np.array([10, -10, 5, -5, 0])
    a = np.random.permutation(np.resize(levels, k // 512 * 4)).reshape(k // 512, 4)
    idx = np.arange(k)
    return np.exp2(a[idx // 512, idx % 128 // 32])


BF16 = ml_dtypes.bfloat16


def bf(x):
    return np.asarray(x, np.float32).astype(BF16)


def f64(x):
    return np.asarray(x).astype(np.float64)


E2M1 = np.array([0.0, 0.5, 1.0, 1.5, 2.0, 3.0, 4.0, 6.0, -0.0, -0.5, -1.0, -1.5, -2.0, -3.0, -4.0, -6.0])


def pack_weight(w, fmt):
    k, n = w.shape
    w = f64(bf(w)).reshape(k // 32, 32, n)
    amax = np.abs(w).max(1)
    if fmt == "e4m3":
        byte = np.frexp(amax)[1] - 1 + 127 - 7
    else:
        mant, ex = np.frexp(amax / 6.0)
        byte = np.where(mant > 0.5, ex, ex - 1) + 127
    byte = np.clip(np.where(amax > 0, byte, 1), 1, 254)
    scaled = (w * np.exp2(127.0 - byte)[:, None, :]).reshape(k, n).astype(np.float32)
    by_word = np.ascontiguousarray(scaled.reshape(k // 512, 128, 4, n).transpose(0, 1, 3, 2))
    if fmt == "e4m3":
        words = by_word.astype(ml_dtypes.float8_e4m3fn).view(np.uint8)
    else:
        c = by_word.astype(ml_dtypes.float4_e2m1fn).view(np.uint8) & 0xF
        words = c[..., 0::2] | (c[..., 1::2] << 4)
    return np.ascontiguousarray(words), np.ascontiguousarray(byte.astype(np.uint8).reshape(k // 512, 16, n))


def unpack_weight(words, scales, fmt):
    g, p, n, _ = words.shape
    if fmt == "e4m3":
        vals = np.ascontiguousarray(words).view(ml_dtypes.float8_e4m3fn).astype(np.float64)
    else:
        nib = np.empty((g, p, n, 4), np.uint8)
        nib[..., 0::2] = words & 0xF
        nib[..., 1::2] = words >> 4
        vals = E2M1[nib]
    vals = vals * np.repeat(np.exp2(scales.astype(np.float64) - 127.0), 8, axis=1)[..., None]
    return vals.transpose(0, 1, 3, 2).reshape(g * 512, n)

def pack4(w):
    words, scales = pack_weight(w, "e2m1")
    return words.reshape(words.shape[0], 128, -1), scales


def unpack4(words, scales):
    return unpack_weight(words.reshape(words.shape[0], 128, -1, 2), scales, "e2m1")


B, S, H, A, NH = 4, 128, 1536, 1536, 12
HD = A // NH
LN_EPS = 1e-5


def setup_inputs():
    s = mx_kscale(A)
    ctx_heads = bf(np.random.standard_normal((B, NH, S, HD)) * s.reshape(NH, 1, HD))
    Wo = np.random.standard_normal((H, A)) / np.sqrt(A) / s
    Wo_words, Wo_scales = pack4(np.ascontiguousarray(Wo.T))
    return {"ctx_heads": ctx_heads,
            "Wo_words": Wo_words,
            "Wo_scales": Wo_scales,
            "bo": bf(np.random.standard_normal(H) * 0.3),
            "features": bf(np.random.standard_normal((B, S, H))),
            "ln_g": bf(1.0 + 0.1 * np.random.standard_normal(H)),
            "ln_b": bf(0.2 * np.random.standard_normal(H))}


def reference(ctx_heads, Wo_words, Wo_scales, bo, features, ln_g, ln_b):
    ctx = f64(ctx_heads).transpose(0, 2, 1, 3).reshape(B, S, A)
    p = (mxq(ctx, 2, "e4m3") @ unpack4(Wo_words, Wo_scales)) + f64(bo)
    y = p + f64(features)
    mu = y.mean(-1, keepdims=True)
    var = y.var(-1, keepdims=True)
    return (y - mu) / np.sqrt(var + LN_EPS) * f64(ln_g) + f64(ln_b)

@@ -1,0 +1,252 @@
+from contextlib import ExitStack
+
+import concourse.mybir as mybir
+from concourse.masks import make_identity
+
+F32 = mybir.dt.float32
+BF16 = mybir.dt.bfloat16
+I32 = mybir.dt.int32
+U32 = mybir.dt.uint32
+U8 = mybir.dt.uint8
+FP8X4 = mybir.dt.float8_e4m3fn_x4
+FP4X4 = mybir.dt.float4_e2m1fn_x4
+ALU = mybir.AluOpType
+ACT = mybir.ActivationFunctionType
+
+P = 128
+PACK = 4
+K_PASS = P * PACK
+BATCH = 4
+HEADS = 12
+HEAD_DIM = 128
+FEAT = 1536
+PASSES = FEAT // K_PASS
+CHUNK = 512
+CHUNKS = FEAT // CHUNK
+LN_EPS = 1e-5
+
+FLOPS = 2 * BATCH * P * FEAT * FEAT
+
+
+def tile_hierarchicalattention_pb_kernel(
+    tc, ctx_heads, Wo_words, Wo_scales, bo, features, ln_g, ln_b, out
+):
+    nc = tc.nc
+    with ExitStack() as stack:
+        keep = stack.enter_context(tc.tile_pool(name="keep", bufs=1))
+        scratch = stack.enter_context(tc.tile_pool(name="scratch", bufs=2))
+        gain_banks = stack.enter_context(tc.psum_pool(name="gain_banks", bufs=1))
+        flip_banks = stack.enter_context(tc.psum_pool(name="flip_banks", bufs=2))
+        acc_banks = stack.enter_context(tc.psum_pool(name="acc_banks", bufs=3))
+        stack.enter_context(tc.manual_schedule())
+
+        x_sb = [keep.tile([P, HEADS, HEAD_DIM], BF16, name="x%d" % b) for b in range(BATCH)]
+        feat = [keep.tile([P, FEAT], BF16, name="feat%d" % b) for b in range(BATCH)]
+        grouped = [
+            keep.tile([P, PASSES * P * PACK], BF16, name="grouped%d" % b, align_bytes=64)
+            for b in range(BATCH)
+        ]
+        x_codes = [
+            keep.tile([P, PASSES * P], U32, name="x_codes%d" % b, align_bytes=64)
+            for b in range(BATCH)
+        ]
+        x_scales = [
+            keep.tile([P, PASSES * P], U8, name="x_scales%d" % b, align_bytes=64)
+            for b in range(BATCH)
+        ]
+        w_words = keep.tile([P, CHUNKS, PASSES, 2 * CHUNK], U8, name="w_words", align_bytes=64)
+        w_scales = keep.tile([P, PASSES, FEAT], U8, name="w_scales", align_bytes=64)
+        resid = [keep.tile([P, FEAT], F32, name="resid%d" % b) for b in range(BATCH)]
+        y = [keep.tile([P, FEAT], F32, name="y%d" % b) for b in range(BATCH)]
+        gained = [keep.tile([P, FEAT], F32, name="gained%d" % b) for b in range(BATCH)]
+        result = [keep.tile([P, FEAT], F32, name="result%d" % b) for b in range(BATCH)]
+        chunk_sums = [keep.tile([P, CHUNKS], F32, name="chunk_sums%d" % b) for b in range(BATCH)]
+        chunk_means = [keep.tile([P, CHUNKS], F32, name="chunk_means%d" % b) for b in range(BATCH)]
+        neg_mean = [keep.tile([P, 1], F32, name="neg_mean%d" % b) for b in range(BATCH)]
+        sum_sq = [keep.tile([P, 1], F32, name="sum_sq%d" % b) for b in range(BATCH)]
+        std = [keep.tile([P, 1], F32, name="std%d" % b) for b in range(BATCH)]
+        rstd = [keep.tile([P, 1], F32, name="rstd%d" % b) for b in range(BATCH)]
+        ident_f32 = keep.tile([P, P], F32, name="ident_f32")
+        ident_bf16 = keep.tile([P, P], BF16, name="ident_bf16")
+        bias_rows = keep.tile([P, CHUNK], BF16, name="bias_rows")
+        affine_rows = keep.tile([P, CHUNK], BF16, name="affine_rows")
+        bias_all = keep.tile([P, FEAT], BF16, name="bias_all")
+        eps = keep.tile([P, 1], F32, name="eps")
+        warm = keep.tile([P, 1], F32, name="warm")
+        gain_shift = [
+            gain_banks.tile([P, 2, CHUNK], BF16, name="gain_shift%d" % c) for c in range(CHUNKS)
+        ]
+
+        nc.vector.memset(bias_rows[:], 0.0)
+        nc.vector.memset(w_scales[:].bitcast(I32), 0)
+        nc.vector.memset(affine_rows[:], 0.0)
+        nc.vector.memset(eps[:], LN_EPS)
+        make_identity(nc, ident_bf16[:])
+        make_identity(nc, ident_f32[:])
+        nc.scalar.activation(out=warm[:], in_=eps[:], func=ACT.Sqrt)
+
+        def load_ctx(b):
+            nc.sync.dma_start(out=x_sb[b][:], in_=ctx_heads[b].rearrange("h s d -> s h d"))
+
+        def load_features(b):
+            nc.sync.dma_start(out=feat[b][:], in_=features[b])
+
+        def load_weight_chunk(c):
+            nc.sync.dma_start(
+                out=w_words[:, c].bitcast(I32),
+                in_=Wo_words.bitcast(I32)[:, :, (CHUNK // 2) * c : (CHUNK // 2) * (c + 1)].rearrange(
+                    "g p n -> p g n"
+                ),
+            )
+
+        def load_rows(rows, first, vector):
+            nc.sync.dma_start(
+                out=rows[first : first + CHUNKS, :], in_=vector.rearrange("(c n) -> c n", c=CHUNKS)
+            )
+
+        load_ctx(0)
+        load_rows(bias_rows, 0, bo)
+        load_features(0)
+        for half in range(2):
+            for r in range(4):
+                nc.sync.dma_start(
+                    out=w_scales[32 * half + r : P : 64].bitcast(I32),
+                    in_=Wo_scales.bitcast(I32)[:, 4 * half + r : 16 : 8, :].rearrange("g q n -> q g n"),
+                )
+        for c in range(CHUNKS):
+            load_weight_chunk(c)
+        load_rows(affine_rows, 0, ln_g)
+        load_rows(affine_rows, CHUNKS, ln_b)
+        for b in range(1, BATCH):
+            load_ctx(b)
+            load_features(b)
+
+        def spread(rows, row, dest):
+            nc.tensor.matmul(
+                out=dest,
+                lhsT=ident_bf16[:, row : row + 1].to_broadcast([P, P]),
+                rhs=rows[:],
+                start=True,
+                stop=True,
+            )
+
+        for c in range(CHUNKS):
+            bias_bank = acc_banks.tile([P, CHUNK], F32, name="bias_bank", tag="acc")
+            spread(bias_rows, c, bias_bank[:])
+            nc.scalar.copy(out=bias_all[:, CHUNK * c : CHUNK * (c + 1)], in_=bias_bank[:])
+
+        def spread_gain_and_shift():
+            for c in range(CHUNKS):
+                spread(affine_rows, c, gain_shift[c][:, 0, :])
+                spread(affine_rows, CHUNKS + c, gain_shift[c][:, 1, :])
+
+        def quantise(b):
+            words = x_sb[b][:].rearrange("s h d -> s (h d)").bitcast(F32)
+            grouped_words = grouped[b][:].bitcast(F32)
+            for g in range(PASSES):
+                flipped = flip_banks.tile([P, 2, P], F32, name="flipped")
+                for u in range(2):
+                    nc.tensor.transpose(
+                        flipped[:, u, :], words[:, 2 * P * g + u : 2 * P * (g + 1) : 2], ident_f32[:]
+                    )
+                nc.scalar.copy(
+                    out=grouped_words[:, 2 * P * g : 2 * P * (g + 1)].rearrange("p (s u) -> p s u", u=2),
+                    in_=flipped[:].rearrange("p u s -> p s u"),
+                )
+            for g in range(PASSES):
+                nc.vector.quantize_mx(
+                    out=x_codes[b][:, P * g : P * (g + 1)].bitcast(FP8X4),
+                    scales=x_scales[b][:, P * g : P * (g + 1)],
+                    in_=grouped[b][:, K_PASS * g : K_PASS * (g + 1)],
+                )
+
+        def residual(b):
+            for c in range(CHUNKS):
+                cols = slice(CHUNK * c, CHUNK * (c + 1))
+                nc.gpsimd.tensor_tensor(
+                    out=resid[b][:, cols], in0=feat[b][:, cols], in1=bias_all[:, cols], op=ALU.add
+                )
+
+        def project(b):
+            for c in range(CHUNKS):
+                cols = slice(CHUNK * c, CHUNK * (c + 1))
+                acc = acc_banks.tile([P, CHUNK], F32, name="acc", tag="acc")
+                for g in range(PASSES):
+                    nc.tensor.matmul_mx(
+                        out=acc[:],
+                        lhsT=x_codes[b][:, P * g : P * (g + 1)].bitcast(FP8X4),
+                        lhsT_scale=x_scales[b][:, P * g : P * (g + 1)],
+                        rhs=w_words[:, c, g, :].bitcast(FP4X4),
+                        rhs_scale=w_scales[:, g, cols],
+                        start=(g == 0),
+                        stop=(g == PASSES - 1),
+                    )
+                nc.vector.scalar_tensor_tensor(
+                    out=y[b][:, cols],
+                    in0=acc[:],
+                    scalar=1.0,
+                    in1=resid[b][:, cols],
+                    op0=ALU.mult,
+                    op1=ALU.add,
+                    accum_out=chunk_sums[b][:, c : c + 1],
+                )
+            nc.vector.tensor_scalar(
+                out=chunk_means[b][:],
+                in0=chunk_sums[b][:],
+                scalar1=-1.0 / FEAT,
+                scalar2=None,
+                op0=ALU.mult,
+                op1=ALU.add,
+                accum_out=neg_mean[b][:],
+            )
+
+        def variance(b):
+            squares = scratch.tile([P, FEAT], F32, name="squares")
+            nc.scalar.activation(
+                out=squares[:], in_=y[b][:], func=ACT.Square, bias=neg_mean[b][:], scale=1.0,
+                accum_out=sum_sq[b][:],
+            )
+            nc.scalar.activation(
+                out=std[b][:], in_=sum_sq[b][:], func=ACT.Sqrt, bias=eps[:], scale=1.0 / FEAT
+            )
+
+        def centre_and_gain(b):
+            for c in range(CHUNKS):
+                cols = slice(CHUNK * c, CHUNK * (c + 1))
+                nc.vector.scalar_tensor_tensor(
+                    out=gained[b][:, cols],
+                    in0=y[b][:, cols],
+                    scalar=neg_mean[b][:],
+                    in1=gain_shift[c][:, 0, :],
+                    op0=ALU.add,
+                    op1=ALU.mult,
+                )
+
+        def scale_shift_store(b):
+            nc.vector.reciprocal(out=rstd[b][:], in_=std[b][:])
+            for c in range(CHUNKS):
+                cols = slice(CHUNK * c, CHUNK * (c + 1))
+                nc.vector.scalar_tensor_tensor(
+                    out=result[b][:, cols],
+                    in0=gained[b][:, cols],
+                    scalar=rstd[b][:],
+                    in1=gain_shift[c][:, 1, :],
+                    op0=ALU.mult,
+                    op1=ALU.add,
+                )
+                nc.sync.dma_start(out=out[b, :, cols], in_=result[b][:, cols])
+
+        quantise(0)
+        residual(0)
+        for b in range(BATCH):
+            project(b)
+            if b == 0:
+                spread_gain_and_shift()
+            centre_and_gain(b)
+            if b + 1 < BATCH:
+                quantise(b + 1)
+                residual(b + 1)
+            variance(b)
+            if b > 0:
+                scale_shift_store(b - 1)
+        scale_shift_store(BATCH - 1)

@@ -21,8 +21,10 @@ HEADS = 12
 HEAD_DIM = 128
 FEAT = 1536
 PASSES = FEAT // K_PASS
+HEADS_PER_PASS = K_PASS // HEAD_DIM
 CHUNK = 512
 CHUNKS = FEAT // CHUNK
+WIDE = 2 * CHUNK
 LN_EPS = 1e-5
 
 FLOPS = 2 * BATCH * P * FEAT * FEAT
@@ -73,9 +75,11 @@ def tile_hierarchicalattention_pb_kernel(
         bias_all = keep.tile([P, FEAT], BF16, name="bias_all")
         eps = keep.tile([P, 1], F32, name="eps")
         warm = keep.tile([P, 1], F32, name="warm")
-        gain_shift = [
-            gain_banks.tile([P, 2, CHUNK], BF16, name="gain_shift%d" % c) for c in range(CHUNKS)
-        ]
+        gain_lo = gain_banks.tile([P, WIDE], BF16, name="gain_lo")
+        gain_hi = gain_banks.tile([P, FEAT - WIDE], BF16, name="gain_hi")
+        shift_lo = gain_banks.tile([P, WIDE], BF16, name="shift_lo")
+        shift_hi = keep.tile([P, FEAT - WIDE], BF16, name="shift_hi")
+        scaled_hi = [keep.tile([P, FEAT - WIDE], F32, name="scaled_hi%d" % b) for b in range(BATCH)]
 
         nc.vector.memset(bias_rows[:], 0.0)
         nc.vector.memset(w_scales[:].bitcast(I32), 0)
@@ -86,7 +90,11 @@ def tile_hierarchicalattention_pb_kernel(
         nc.scalar.activation(out=warm[:], in_=eps[:], func=ACT.Sqrt)
 
         def load_ctx(b):
-            nc.sync.dma_start(out=x_sb[b][:], in_=ctx_heads[b].rearrange("h s d -> s h d"))
+            for g in range(PASSES):
+                heads = slice(HEADS_PER_PASS * g, HEADS_PER_PASS * (g + 1))
+                nc.sync.dma_start(
+                    out=x_sb[b][:, heads, :], in_=ctx_heads[b, heads].rearrange("h s d -> s h d")
+                )
 
         def load_features(b):
             nc.sync.dma_start(out=feat[b][:], in_=features[b])
@@ -107,19 +115,20 @@ def tile_hierarchicalattention_pb_kernel(
         load_ctx(0)
         load_rows(bias_rows, 0, bo)
         load_features(0)
-        for half in range(2):
-            for r in range(4):
-                nc.sync.dma_start(
-                    out=w_scales[32 * half + r : P : 64].bitcast(I32),
-                    in_=Wo_scales.bitcast(I32)[:, 4 * half + r : 16 : 8, :].rearrange("g q n -> q g n"),
-                )
+        for r in range(4):
+            nc.sync.dma_start(
+                out=w_scales[r : P : 32].bitcast(I32),
+                in_=Wo_scales.bitcast(I32)[:, r : 16 : 4, :].rearrange("g q n -> q g n"),
+            )
         for c in range(CHUNKS):
             load_weight_chunk(c)
         load_rows(affine_rows, 0, ln_g)
         load_rows(affine_rows, CHUNKS, ln_b)
-        for b in range(1, BATCH):
+        load_ctx(1)
+        for b in range(2, BATCH):
             load_ctx(b)
-            load_features(b)
+            load_features(b - 1)
+        load_features(BATCH - 1)
 
         def spread(rows, row, dest):
             nc.tensor.matmul(
@@ -130,15 +139,23 @@ def tile_hierarchicalattention_pb_kernel(
                 stop=True,
             )
 
-        for c in range(CHUNKS):
-            bias_bank = acc_banks.tile([P, CHUNK], F32, name="bias_bank", tag="acc")
-            spread(bias_rows, c, bias_bank[:])
-            nc.scalar.copy(out=bias_all[:, CHUNK * c : CHUNK * (c + 1)], in_=bias_bank[:])
-
-        def spread_gain_and_shift():
+        def spread_bias():
             for c in range(CHUNKS):
-                spread(affine_rows, c, gain_shift[c][:, 0, :])
-                spread(affine_rows, CHUNKS + c, gain_shift[c][:, 1, :])
+                bias_bank = acc_banks.tile([P, CHUNK], F32, name="bias_bank", tag="acc")
+                spread(bias_rows, c, bias_bank[:])
+                nc.scalar.copy(out=bias_all[:, CHUNK * c : CHUNK * (c + 1)], in_=bias_bank[:])
+
+        def spread_gain():
+            spread(affine_rows, 0, gain_lo[:, :CHUNK])
+            spread(affine_rows, 1, gain_lo[:, CHUNK:])
+            spread(affine_rows, 2, gain_hi[:])
+
+        def spread_shift():
+            spread(affine_rows, CHUNKS, shift_lo[:, :CHUNK])
+            spread(affine_rows, CHUNKS + 1, shift_lo[:, CHUNK:])
+            shift_bank = acc_banks.tile([P, CHUNK], F32, name="shift_bank", tag="acc")
+            spread(affine_rows, CHUNKS + 2, shift_bank[:])
+            nc.scalar.copy(out=shift_hi[:], in_=shift_bank[:])
 
         def quantise(b):
             words = x_sb[b][:].rearrange("s h d -> s (h d)").bitcast(F32)
@@ -211,42 +228,54 @@ def tile_hierarchicalattention_pb_kernel(
             )
 
         def centre_and_gain(b):
-            for c in range(CHUNKS):
-                cols = slice(CHUNK * c, CHUNK * (c + 1))
+            for cols, gain in ((slice(0, WIDE), gain_lo), (slice(WIDE, FEAT), gain_hi)):
                 nc.vector.scalar_tensor_tensor(
                     out=gained[b][:, cols],
                     in0=y[b][:, cols],
                     scalar=neg_mean[b][:],
-                    in1=gain_shift[c][:, 0, :],
+                    in1=gain[:],
                     op0=ALU.add,
                     op1=ALU.mult,
                 )
 
-        def scale_shift_store(b):
+        def shift_wide(b):
             nc.vector.reciprocal(out=rstd[b][:], in_=std[b][:])
-            for c in range(CHUNKS):
-                cols = slice(CHUNK * c, CHUNK * (c + 1))
-                nc.vector.scalar_tensor_tensor(
-                    out=result[b][:, cols],
-                    in0=gained[b][:, cols],
-                    scalar=rstd[b][:],
-                    in1=gain_shift[c][:, 1, :],
-                    op0=ALU.mult,
-                    op1=ALU.add,
-                )
-                nc.sync.dma_start(out=out[b, :, cols], in_=result[b][:, cols])
+            nc.vector.scalar_tensor_tensor(
+                out=result[b][:, :WIDE],
+                in0=gained[b][:, :WIDE],
+                scalar=rstd[b][:],
+                in1=shift_lo[:],
+                op0=ALU.mult,
+                op1=ALU.add,
+            )
+            nc.sync.dma_start(out=out[b, :, :WIDE], in_=result[b][:, :WIDE])
+
+        def shift_narrow(b):
+            nc.scalar.activation(
+                out=scaled_hi[b][:], in_=gained[b][:, WIDE:], func=ACT.Copy, scale=rstd[b][:]
+            )
+            nc.gpsimd.tensor_tensor(
+                out=result[b][:, WIDE:], in0=scaled_hi[b][:], in1=shift_hi[:], op=ALU.add
+            )
+            nc.sync.dma_start(out=out[b, :, WIDE:], in_=result[b][:, WIDE:])
 
         quantise(0)
-        residual(0)
+        spread_bias()
+        for b in range(BATCH):
+            residual(b)
         for b in range(BATCH):
             project(b)
             if b == 0:
-                spread_gain_and_shift()
+                spread_gain()
+            if b == 1:
+                spread_shift()
+            if b > 0:
+                shift_wide(b - 1)
             centre_and_gain(b)
-            if b + 1 < BATCH:
-                quantise(b + 1)
-                residual(b + 1)
+            for ahead in range(1 if b == 0 else b + 2, min(b + 3, BATCH)):
+                quantise(ahead)
             variance(b)
             if b > 0:
-                scale_shift_store(b - 1)
-        scale_shift_store(BATCH - 1)
+                shift_narrow(b - 1)
+        shift_wide(BATCH - 1)
+        shift_narrow(BATCH - 1)

@@ -66,7 +66,6 @@ def tile_hierarchicalattention_pb_kernel(
         chunk_means = [keep.tile([P, CHUNKS], F32, name="chunk_means%d" % b) for b in range(BATCH)]
         neg_mean = [keep.tile([P, 1], F32, name="neg_mean%d" % b) for b in range(BATCH)]
         sum_sq = [keep.tile([P, 1], F32, name="sum_sq%d" % b) for b in range(BATCH)]
-        std = [keep.tile([P, 1], F32, name="std%d" % b) for b in range(BATCH)]
         rstd = [keep.tile([P, 1], F32, name="rstd%d" % b) for b in range(BATCH)]
         ident_f32 = keep.tile([P, P], F32, name="ident_f32")
         ident_bf16 = keep.tile([P, P], BF16, name="ident_bf16")
@@ -87,7 +86,7 @@ def tile_hierarchicalattention_pb_kernel(
         nc.vector.memset(eps[:], LN_EPS)
         make_identity(nc, ident_bf16[:])
         make_identity(nc, ident_f32[:])
-        nc.scalar.activation(out=warm[:], in_=eps[:], func=ACT.Sqrt)
+        nc.scalar.activation(out=warm[:], in_=eps[:], func=ACT.Abs_reciprocal_sqrt)
 
         def load_ctx(b):
             for g in range(PASSES):
@@ -124,11 +123,11 @@ def tile_hierarchicalattention_pb_kernel(
             load_weight_chunk(c)
         load_rows(affine_rows, 0, ln_g)
         load_rows(affine_rows, CHUNKS, ln_b)
+        load_features(1)
         load_ctx(1)
         for b in range(2, BATCH):
             load_ctx(b)
-            load_features(b - 1)
-        load_features(BATCH - 1)
+            load_features(b)
 
         def spread(rows, row, dest):
             nc.tensor.matmul(
@@ -150,12 +149,14 @@ def tile_hierarchicalattention_pb_kernel(
             spread(affine_rows, 1, gain_lo[:, CHUNK:])
             spread(affine_rows, 2, gain_hi[:])
 
-        def spread_shift():
-            spread(affine_rows, CHUNKS, shift_lo[:, :CHUNK])
-            spread(affine_rows, CHUNKS + 1, shift_lo[:, CHUNK:])
+        def spread_shift_narrow():
             shift_bank = acc_banks.tile([P, CHUNK], F32, name="shift_bank", tag="acc")
             spread(affine_rows, CHUNKS + 2, shift_bank[:])
             nc.scalar.copy(out=shift_hi[:], in_=shift_bank[:])
+
+        def spread_shift_wide():
+            spread(affine_rows, CHUNKS, shift_lo[:, :CHUNK])
+            spread(affine_rows, CHUNKS + 1, shift_lo[:, CHUNK:])
 
         def quantise(b):
             words = x_sb[b][:].rearrange("s h d -> s (h d)").bitcast(F32)
@@ -170,17 +171,17 @@ def tile_hierarchicalattention_pb_kernel(
                     out=grouped_words[:, 2 * P * g : 2 * P * (g + 1)].rearrange("p (s u) -> p s u", u=2),
                     in_=flipped[:].rearrange("p u s -> p s u"),
                 )
-            for g in range(PASSES):
+            for first, count in ((0, 2), (2, 1)):
                 nc.vector.quantize_mx(
-                    out=x_codes[b][:, P * g : P * (g + 1)].bitcast(FP8X4),
-                    scales=x_scales[b][:, P * g : P * (g + 1)],
-                    in_=grouped[b][:, K_PASS * g : K_PASS * (g + 1)],
+                    out=x_codes[b][:, P * first : P * (first + count)].bitcast(FP8X4),
+                    scales=x_scales[b][:, P * first : P * (first + count)],
+                    in_=grouped[b][:, K_PASS * first : K_PASS * (first + count)],
                 )
 
-        def residual(b):
+        def residual(engine, b):
             for c in range(CHUNKS):
                 cols = slice(CHUNK * c, CHUNK * (c + 1))
-                nc.gpsimd.tensor_tensor(
+                engine.tensor_tensor(
                     out=resid[b][:, cols], in0=feat[b][:, cols], in1=bias_all[:, cols], op=ALU.add
                 )
 
@@ -207,13 +208,8 @@ def tile_hierarchicalattention_pb_kernel(
                     op1=ALU.add,
                     accum_out=chunk_sums[b][:, c : c + 1],
                 )
-            nc.vector.tensor_scalar(
-                out=chunk_means[b][:],
-                in0=chunk_sums[b][:],
-                scalar1=-1.0 / FEAT,
-                scalar2=None,
-                op0=ALU.mult,
-                op1=ALU.add,
+            nc.scalar.activation(
+                out=chunk_means[b][:], in_=chunk_sums[b][:], func=ACT.Copy, scale=-1.0 / FEAT,
                 accum_out=neg_mean[b][:],
             )
 
@@ -224,11 +220,12 @@ def tile_hierarchicalattention_pb_kernel(
                 accum_out=sum_sq[b][:],
             )
             nc.scalar.activation(
-                out=std[b][:], in_=sum_sq[b][:], func=ACT.Sqrt, bias=eps[:], scale=1.0 / FEAT
+                out=rstd[b][:], in_=sum_sq[b][:], func=ACT.Abs_reciprocal_sqrt, bias=eps[:],
+                scale=1.0 / FEAT,
             )
 
         def centre_and_gain(b):
-            for cols, gain in ((slice(0, WIDE), gain_lo), (slice(WIDE, FEAT), gain_hi)):
+            for cols, gain in ((slice(WIDE, FEAT), gain_hi), (slice(0, WIDE), gain_lo)):
                 nc.vector.scalar_tensor_tensor(
                     out=gained[b][:, cols],
                     in0=y[b][:, cols],
@@ -239,7 +236,6 @@ def tile_hierarchicalattention_pb_kernel(
                 )
 
         def shift_wide(b):
-            nc.vector.reciprocal(out=rstd[b][:], in_=std[b][:])
             nc.vector.scalar_tensor_tensor(
                 out=result[b][:, :WIDE],
                 in0=gained[b][:, :WIDE],
@@ -261,21 +257,21 @@ def tile_hierarchicalattention_pb_kernel(
 
         quantise(0)
         spread_bias()
-        for b in range(BATCH):
-            residual(b)
+        residual(nc.vector, 0)
+        for b in range(1, BATCH):
+            residual(nc.gpsimd, b)
         for b in range(BATCH):
             project(b)
             if b == 0:
                 spread_gain()
+                spread_shift_narrow()
             if b == 1:
-                spread_shift()
+                spread_shift_wide()
             if b > 0:
                 shift_wide(b - 1)
             centre_and_gain(b)
             for ahead in range(1 if b == 0 else b + 2, min(b + 3, BATCH)):
                 quantise(ahead)
             variance(b)
-            if b > 0:
-                shift_narrow(b - 1)
+            shift_narrow(b)
         shift_wide(BATCH - 1)
-        shift_narrow(BATCH - 1)

@@ -113,6 +113,8 @@ def tile_hierarchicalattention_pb_kernel(
 
         load_ctx(0)
         load_rows(bias_rows, 0, bo)
+        load_rows(affine_rows, 0, ln_g)
+        load_rows(affine_rows, CHUNKS, ln_b)
         load_features(0)
         for r in range(4):
             nc.sync.dma_start(
@@ -121,11 +123,7 @@ def tile_hierarchicalattention_pb_kernel(
             )
         for c in range(CHUNKS):
             load_weight_chunk(c)
-        load_rows(affine_rows, 0, ln_g)
-        load_rows(affine_rows, CHUNKS, ln_b)
-        load_features(1)
-        load_ctx(1)
-        for b in range(2, BATCH):
+        for b in range(1, BATCH):
             load_ctx(b)
             load_features(b)
 
@@ -235,16 +233,18 @@ def tile_hierarchicalattention_pb_kernel(
                     op1=ALU.mult,
                 )
 
-        def shift_wide(b):
-            nc.vector.scalar_tensor_tensor(
-                out=result[b][:, :WIDE],
-                in0=gained[b][:, :WIDE],
-                scalar=rstd[b][:],
-                in1=shift_lo[:],
-                op0=ALU.mult,
-                op1=ALU.add,
-            )
-            nc.sync.dma_start(out=out[b, :, :WIDE], in_=result[b][:, :WIDE])
+        def shift_wide(b, pieces):
+            for i in range(pieces):
+                cols = slice(WIDE // pieces * i, WIDE // pieces * (i + 1))
+                nc.vector.scalar_tensor_tensor(
+                    out=result[b][:, cols],
+                    in0=gained[b][:, cols],
+                    scalar=rstd[b][:],
+                    in1=shift_lo[:, cols],
+                    op0=ALU.mult,
+                    op1=ALU.add,
+                )
+                nc.sync.dma_start(out=out[b, :, cols], in_=result[b][:, cols])
 
         def shift_narrow(b):
             nc.scalar.activation(
@@ -257,21 +257,20 @@ def tile_hierarchicalattention_pb_kernel(
 
         quantise(0)
         spread_bias()
+        spread_gain()
+        spread_shift_narrow()
         residual(nc.vector, 0)
         for b in range(1, BATCH):
             residual(nc.gpsimd, b)
         for b in range(BATCH):
             project(b)
             if b == 0:
-                spread_gain()
-                spread_shift_narrow()
-            if b == 1:
                 spread_shift_wide()
             if b > 0:
-                shift_wide(b - 1)
+                shift_wide(b - 1, 1)
             centre_and_gain(b)
             for ahead in range(1 if b == 0 else b + 2, min(b + 3, BATCH)):
                 quantise(ahead)
             variance(b)
             shift_narrow(b)
-        shift_wide(BATCH - 1)
+        shift_wide(BATCH - 1, 2)

@@ -113,8 +113,6 @@ def tile_hierarchicalattention_pb_kernel(
 
         load_ctx(0)
         load_rows(bias_rows, 0, bo)
-        load_rows(affine_rows, 0, ln_g)
-        load_rows(affine_rows, CHUNKS, ln_b)
         load_features(0)
         for r in range(4):
             nc.sync.dma_start(
@@ -123,7 +121,11 @@ def tile_hierarchicalattention_pb_kernel(
             )
         for c in range(CHUNKS):
             load_weight_chunk(c)
-        for b in range(1, BATCH):
+        load_rows(affine_rows, 0, ln_g)
+        load_rows(affine_rows, CHUNKS, ln_b)
+        load_features(1)
+        load_ctx(1)
+        for b in range(2, BATCH):
             load_ctx(b)
             load_features(b)
 
@@ -159,17 +161,22 @@ def tile_hierarchicalattention_pb_kernel(
         def quantise(b):
             words = x_sb[b][:].rearrange("s h d -> s (h d)").bitcast(F32)
             grouped_words = grouped[b][:].bitcast(F32)
-            for g in range(PASSES):
-                flipped = flip_banks.tile([P, 2, P], F32, name="flipped")
-                for u in range(2):
-                    nc.tensor.transpose(
-                        flipped[:, u, :], words[:, 2 * P * g + u : 2 * P * (g + 1) : 2], ident_f32[:]
-                    )
-                nc.scalar.copy(
-                    out=grouped_words[:, 2 * P * g : 2 * P * (g + 1)].rearrange("p (s u) -> p s u", u=2),
-                    in_=flipped[:].rearrange("p u s -> p s u"),
-                )
             for first, count in ((0, 2), (2, 1)):
+                flipped = flip_banks.tile([P, 2 * count, P], F32, name="flipped")
+                for j in range(count):
+                    g = first + j
+                    for u in range(2):
+                        nc.tensor.transpose(
+                            flipped[:, 2 * j + u, :],
+                            words[:, 2 * P * g + u : 2 * P * (g + 1) : 2],
+                            ident_f32[:],
+                        )
+                nc.scalar.copy(
+                    out=grouped_words[:, 2 * P * first : 2 * P * (first + count)].rearrange(
+                        "p (j s u) -> p j s u", j=count, u=2
+                    ),
+                    in_=flipped[:].rearrange("p (j u) s -> p j s u", u=2),
+                )
                 nc.vector.quantize_mx(
                     out=x_codes[b][:, P * first : P * (first + count)].bitcast(FP8X4),
                     scales=x_scales[b][:, P * first : P * (first + count)],
@@ -257,14 +264,15 @@ def tile_hierarchicalattention_pb_kernel(
 
         quantise(0)
         spread_bias()
-        spread_gain()
-        spread_shift_narrow()
         residual(nc.vector, 0)
         for b in range(1, BATCH):
             residual(nc.gpsimd, b)
         for b in range(BATCH):
             project(b)
             if b == 0:
+                spread_gain()
+                spread_shift_narrow()
+            if b == 1:
                 spread_shift_wide()
             if b > 0:
                 shift_wide(b - 1, 1)

@@ -206,9 +206,9 @@ def tile_hierarchicalattention_pb_kernel(
                     )
                 nc.vector.scalar_tensor_tensor(
                     out=y[b][:, cols],
-                    in0=acc[:],
+                    in0=resid[b][:, cols],
                     scalar=1.0,
-                    in1=resid[b][:, cols],
+                    in1=acc[:],
                     op0=ALU.mult,
                     op1=ALU.add,
                     accum_out=chunk_sums[b][:, c : c + 1],

@@ -26,6 +26,7 @@ CHUNK = 512
 CHUNKS = FEAT // CHUNK
 WIDE = 2 * CHUNK
 LN_EPS = 1e-5
+NARROW = (512, 1024, 1024, 256)
 
 FLOPS = 2 * BATCH * P * FEAT * FEAT
 
@@ -38,8 +39,7 @@ def tile_hierarchicalattention_pb_kernel(
         keep = stack.enter_context(tc.tile_pool(name="keep", bufs=1))
         scratch = stack.enter_context(tc.tile_pool(name="scratch", bufs=2))
         gain_banks = stack.enter_context(tc.psum_pool(name="gain_banks", bufs=1))
-        flip_banks = stack.enter_context(tc.psum_pool(name="flip_banks", bufs=2))
-        acc_banks = stack.enter_context(tc.psum_pool(name="acc_banks", bufs=3))
+        acc_banks = stack.enter_context(tc.psum_pool(name="acc_banks", bufs=5))
         stack.enter_context(tc.manual_schedule())
 
         x_sb = [keep.tile([P, HEADS, HEAD_DIM], BF16, name="x%d" % b) for b in range(BATCH)]
@@ -75,10 +75,12 @@ def tile_hierarchicalattention_pb_kernel(
         eps = keep.tile([P, 1], F32, name="eps")
         warm = keep.tile([P, 1], F32, name="warm")
         gain_lo = gain_banks.tile([P, WIDE], BF16, name="gain_lo")
-        gain_hi = gain_banks.tile([P, FEAT - WIDE], BF16, name="gain_hi")
+        both_hi = gain_banks.tile([P, 2 * (FEAT - WIDE)], BF16, name="both_hi")
+        gain_hi = both_hi[:, : FEAT - WIDE]
+        shift_hi = both_hi[:, FEAT - WIDE :]
         shift_lo = gain_banks.tile([P, WIDE], BF16, name="shift_lo")
-        shift_hi = keep.tile([P, FEAT - WIDE], BF16, name="shift_hi")
-        scaled_hi = [keep.tile([P, FEAT - WIDE], F32, name="scaled_hi%d" % b) for b in range(BATCH)]
+        shift_sb = keep.tile([P, FEAT], BF16, name="shift_sb")
+        scaled = [keep.tile([P, FEAT], F32, name="scaled%d" % b) for b in range(BATCH)]
 
         nc.vector.memset(bias_rows[:], 0.0)
         nc.vector.memset(w_scales[:].bitcast(I32), 0)
@@ -147,22 +149,27 @@ def tile_hierarchicalattention_pb_kernel(
         def spread_gain():
             spread(affine_rows, 0, gain_lo[:, :CHUNK])
             spread(affine_rows, 1, gain_lo[:, CHUNK:])
-            spread(affine_rows, 2, gain_hi[:])
+            spread(affine_rows, 2, gain_hi)
 
-        def spread_shift_narrow():
-            shift_bank = acc_banks.tile([P, CHUNK], F32, name="shift_bank", tag="acc")
-            spread(affine_rows, CHUNKS + 2, shift_bank[:])
-            nc.scalar.copy(out=shift_hi[:], in_=shift_bank[:])
-
-        def spread_shift_wide():
+        def spread_shift():
+            spread(affine_rows, CHUNKS + 2, shift_hi)
             spread(affine_rows, CHUNKS, shift_lo[:, :CHUNK])
             spread(affine_rows, CHUNKS + 1, shift_lo[:, CHUNK:])
+
+        def shift_in_psum(cols):
+            if cols.start >= WIDE:
+                return shift_hi[:, cols.start - WIDE : cols.stop - WIDE]
+            return shift_lo[:, cols]
+
+        def shift_to_sbuf(c):
+            cols = slice(CHUNK * c, CHUNK * (c + 1))
+            nc.scalar.copy(out=shift_sb[:, cols], in_=shift_in_psum(cols))
 
         def quantise(b):
             words = x_sb[b][:].rearrange("s h d -> s (h d)").bitcast(F32)
             grouped_words = grouped[b][:].bitcast(F32)
             for first, count in ((0, 2), (2, 1)):
-                flipped = flip_banks.tile([P, 2 * count, P], F32, name="flipped")
+                flipped = acc_banks.tile([P, 2 * count, P], F32, name="flipped", tag="acc")
                 for j in range(count):
                     g = first + j
                     for u in range(2):
@@ -230,37 +237,43 @@ def tile_hierarchicalattention_pb_kernel(
             )
 
         def centre_and_gain(b):
-            for cols, gain in ((slice(WIDE, FEAT), gain_hi), (slice(0, WIDE), gain_lo)):
+            for cols, gain in ((slice(WIDE, FEAT), gain_hi), (slice(0, WIDE), gain_lo[:])):
                 nc.vector.scalar_tensor_tensor(
                     out=gained[b][:, cols],
                     in0=y[b][:, cols],
                     scalar=neg_mean[b][:],
-                    in1=gain[:],
+                    in1=gain,
                     op0=ALU.add,
                     op1=ALU.mult,
                 )
 
-        def shift_wide(b, pieces):
-            for i in range(pieces):
-                cols = slice(WIDE // pieces * i, WIDE // pieces * (i + 1))
+        def shift_wide(b, step):
+            last = FEAT - NARROW[b]
+            for first in range(0, last, step):
+                cols = slice(first, min(first + step, last))
                 nc.vector.scalar_tensor_tensor(
                     out=result[b][:, cols],
                     in0=gained[b][:, cols],
                     scalar=rstd[b][:],
-                    in1=shift_lo[:, cols],
+                    in1=shift_in_psum(cols),
                     op0=ALU.mult,
                     op1=ALU.add,
                 )
                 nc.sync.dma_start(out=out[b, :, cols], in_=result[b][:, cols])
 
         def shift_narrow(b):
-            nc.scalar.activation(
-                out=scaled_hi[b][:], in_=gained[b][:, WIDE:], func=ACT.Copy, scale=rstd[b][:]
-            )
-            nc.gpsimd.tensor_tensor(
-                out=result[b][:, WIDE:], in0=scaled_hi[b][:], in1=shift_hi[:], op=ALU.add
-            )
-            nc.sync.dma_start(out=out[b, :, WIDE:], in_=result[b][:, WIDE:])
+            for stop in range(FEAT, FEAT - NARROW[b], -CHUNK):
+                cols = slice(max(stop - CHUNK, FEAT - NARROW[b]), stop)
+                nc.scalar.activation(
+                    out=scaled[b][:, cols], in_=gained[b][:, cols], func=ACT.Copy, scale=rstd[b][:]
+                )
+                nc.gpsimd.tensor_tensor(
+                    out=result[b][:, cols], in0=scaled[b][:, cols], in1=shift_sb[:, cols], op=ALU.add
+                )
+
+        def store_narrow(b):
+            first = FEAT - NARROW[b]
+            nc.sync.dma_start(out=out[b, :, first:], in_=result[b][:, first:])
 
         quantise(0)
         spread_bias()
@@ -268,17 +281,26 @@ def tile_hierarchicalattention_pb_kernel(
         for b in range(1, BATCH):
             residual(nc.gpsimd, b)
         for b in range(BATCH):
+            if b == 1:
+                shift_to_sbuf(2)
+            if b == 2:
+                shift_to_sbuf(1)
+            if b > 0:
+                shift_narrow(b - 1)
             project(b)
             if b == 0:
                 spread_gain()
-                spread_shift_narrow()
-            if b == 1:
-                spread_shift_wide()
             if b > 0:
-                shift_wide(b - 1, 1)
+                shift_wide(b - 1, WIDE)
+            if b > 1:
+                store_narrow(b - 2)
             centre_and_gain(b)
             for ahead in range(1 if b == 0 else b + 2, min(b + 3, BATCH)):
                 quantise(ahead)
+            if b == 0:
+                spread_shift()
             variance(b)
-            shift_narrow(b)
-        shift_wide(BATCH - 1, 2)
+        shift_narrow(BATCH - 1)
+        store_narrow(BATCH - 2)
+        shift_wide(BATCH - 1, CHUNK)
+        store_narrow(BATCH - 1)

@@ -115,13 +115,14 @@ def tile_hierarchicalattention_pb_kernel(
 
         load_ctx(0)
         load_rows(bias_rows, 0, bo)
-        load_features(0)
         for r in range(4):
             nc.sync.dma_start(
                 out=w_scales[r : P : 32].bitcast(I32),
                 in_=Wo_scales.bitcast(I32)[:, r : 16 : 4, :].rearrange("g q n -> q g n"),
             )
-        for c in range(CHUNKS):
+        load_weight_chunk(0)
+        load_features(0)
+        for c in range(1, CHUNKS):
             load_weight_chunk(c)
         load_rows(affine_rows, 0, ln_g)
         load_rows(affine_rows, CHUNKS, ln_b)

@@ -295,9 +295,13 @@ def tile_hierarchicalattention_pb_kernel(
                 shift_wide(b - 1, WIDE)
             if b > 1:
                 store_narrow(b - 2)
+            if b == 1:
+                quantise(2)
             centre_and_gain(b)
-            for ahead in range(1 if b == 0 else b + 2, min(b + 3, BATCH)):
-                quantise(ahead)
+            if b == 0:
+                quantise(1)
+            if b == 1:
+                quantise(3)
             if b == 0:
                 spread_shift()
             variance(b)

@@ -237,16 +237,19 @@ def tile_hierarchicalattention_pb_kernel(
                 scale=1.0 / FEAT,
             )
 
+        def gain_cols(b, cols, gain):
+            nc.vector.scalar_tensor_tensor(
+                out=gained[b][:, cols],
+                in0=y[b][:, cols],
+                scalar=neg_mean[b][:],
+                in1=gain,
+                op0=ALU.add,
+                op1=ALU.mult,
+            )
+
         def centre_and_gain(b):
-            for cols, gain in ((slice(WIDE, FEAT), gain_hi), (slice(0, WIDE), gain_lo[:])):
-                nc.vector.scalar_tensor_tensor(
-                    out=gained[b][:, cols],
-                    in0=y[b][:, cols],
-                    scalar=neg_mean[b][:],
-                    in1=gain,
-                    op0=ALU.add,
-                    op1=ALU.mult,
-                )
+            gain_cols(b, slice(WIDE, FEAT), gain_hi)
+            gain_cols(b, slice(0, WIDE), gain_lo[:])
 
         def shift_wide(b, step):
             last = FEAT - NARROW[b]
@@ -273,8 +276,9 @@ def tile_hierarchicalattention_pb_kernel(
                 )
 
         def store_narrow(b):
-            first = FEAT - NARROW[b]
-            nc.sync.dma_start(out=out[b, :, first:], in_=result[b][:, first:])
+            for stop in range(FEAT, FEAT - NARROW[b], -CHUNK):
+                cols = slice(max(stop - CHUNK, FEAT - NARROW[b]), stop)
+                nc.sync.dma_start(out=out[b, :, cols], in_=result[b][:, cols])
 
         quantise(0)
         spread_bias()
@@ -297,9 +301,13 @@ def tile_hierarchicalattention_pb_kernel(
                 store_narrow(b - 2)
             if b == 1:
                 quantise(2)
-            centre_and_gain(b)
             if b == 0:
+                gain_cols(b, slice(WIDE, FEAT), gain_hi)
+                gain_cols(b, slice(0, CHUNK), gain_lo[:, :CHUNK])
                 quantise(1)
+                gain_cols(b, slice(CHUNK, WIDE), gain_lo[:, CHUNK:])
+            else:
+                centre_and_gain(b)
             if b == 1:
                 quantise(3)
             if b == 0:

@@ -26,7 +26,6 @@ CHUNK = 512
 CHUNKS = FEAT // CHUNK
 WIDE = 2 * CHUNK
 LN_EPS = 1e-5
-NARROW = (512, 1024, 1024, 256)
 
 FLOPS = 2 * BATCH * P * FEAT * FEAT
 
@@ -39,9 +38,10 @@ def tile_hierarchicalattention_pb_kernel(
         keep = stack.enter_context(tc.tile_pool(name="keep", bufs=1))
         scratch = stack.enter_context(tc.tile_pool(name="scratch", bufs=2))
         gain_banks = stack.enter_context(tc.psum_pool(name="gain_banks", bufs=1))
-        acc_banks = stack.enter_context(tc.psum_pool(name="acc_banks", bufs=5))
+        acc_banks = stack.enter_context(tc.psum_pool(name="acc_banks", bufs=6))
         stack.enter_context(tc.manual_schedule())
 
+        x_pair = keep.tile([P, HEADS, 2, HEAD_DIM], BF16, name="x_pair")
         x_sb = [keep.tile([P, HEADS, HEAD_DIM], BF16, name="x%d" % b) for b in range(BATCH)]
         feat = [keep.tile([P, FEAT], BF16, name="feat%d" % b) for b in range(BATCH)]
         grouped = [
@@ -66,6 +66,11 @@ def tile_hierarchicalattention_pb_kernel(
         chunk_means = [keep.tile([P, CHUNKS], F32, name="chunk_means%d" % b) for b in range(BATCH)]
         neg_mean = [keep.tile([P, 1], F32, name="neg_mean%d" % b) for b in range(BATCH)]
         sum_sq = [keep.tile([P, 1], F32, name="sum_sq%d" % b) for b in range(BATCH)]
+        first_mean = [keep.tile([P, 1], F32, name="first_mean%d" % b) for b in range(BATCH)]
+        chunk_sq = [keep.tile([P, CHUNKS], F32, name="chunk_sq%d" % b) for b in range(BATCH)]
+        chunk_vars = [keep.tile([P, CHUNKS], F32, name="chunk_vars%d" % b) for b in range(BATCH)]
+        mean_gap = [keep.tile([P, 1], F32, name="mean_gap%d" % b) for b in range(BATCH)]
+        eps_gap = [keep.tile([P, 1], F32, name="eps_gap%d" % b) for b in range(BATCH)]
         rstd = [keep.tile([P, 1], F32, name="rstd%d" % b) for b in range(BATCH)]
         ident_f32 = keep.tile([P, P], F32, name="ident_f32")
         ident_bf16 = keep.tile([P, P], BF16, name="ident_bf16")
@@ -77,10 +82,10 @@ def tile_hierarchicalattention_pb_kernel(
         gain_lo = gain_banks.tile([P, WIDE], BF16, name="gain_lo")
         both_hi = gain_banks.tile([P, 2 * (FEAT - WIDE)], BF16, name="both_hi")
         gain_hi = both_hi[:, : FEAT - WIDE]
-        shift_hi = both_hi[:, FEAT - WIDE :]
-        shift_lo = gain_banks.tile([P, WIDE], BF16, name="shift_lo")
+        shift_first = both_hi[:, FEAT - WIDE :]
         shift_sb = keep.tile([P, FEAT], BF16, name="shift_sb")
         scaled = [keep.tile([P, FEAT], F32, name="scaled%d" % b) for b in range(BATCH)]
+        rstd_diag = [keep.tile([P, P], F32, name="rstd_diag%d" % b) for b in range(BATCH)]
 
         nc.vector.memset(bias_rows[:], 0.0)
         nc.vector.memset(w_scales[:].bitcast(I32), 0)
@@ -90,15 +95,34 @@ def tile_hierarchicalattention_pb_kernel(
         make_identity(nc, ident_f32[:])
         nc.scalar.activation(out=warm[:], in_=eps[:], func=ACT.Abs_reciprocal_sqrt)
 
-        def load_ctx(b):
-            for g in range(PASSES):
-                heads = slice(HEADS_PER_PASS * g, HEADS_PER_PASS * (g + 1))
+        def load_ctx_pair(first, stop):
+            heads = slice(first, stop)
+            for b in range(2):
+                nc.sync.dma_start(
+                    out=x_pair[b : P : 2, heads],
+                    in_=ctx_heads[b, heads].rearrange("h (i e) d -> i h e d", e=2),
+                )
+
+        def split_pair(copy, e, first, stop):
+            heads = slice(first, stop)
+            copy(out=x_sb[e][:, heads, :], in_=x_pair[:, heads, e, :])
+
+        def load_ctx(b, *bounds):
+            for first, stop in zip((0,) + bounds, bounds + (HEADS,)):
+                heads = slice(first, stop)
                 nc.sync.dma_start(
                     out=x_sb[b][:, heads, :], in_=ctx_heads[b, heads].rearrange("h s d -> s h d")
                 )
 
-        def load_features(b):
-            nc.sync.dma_start(out=feat[b][:], in_=features[b])
+        def load_features(t):
+            if t < 2:
+                for b in range(2):
+                    nc.sync.dma_start(
+                        out=feat[t][b : P : 2, :],
+                        in_=features[b].rearrange("(i e) n -> e i n", e=2)[t],
+                    )
+            else:
+                nc.sync.dma_start(out=feat[t][:], in_=features[t])
 
         def load_weight_chunk(c):
             nc.sync.dma_start(
@@ -108,119 +132,131 @@ def tile_hierarchicalattention_pb_kernel(
                 ),
             )
 
+        def load_weight_scales():
+            for r in range(4):
+                nc.sync.dma_start(
+                    out=w_scales[r : P : 32].bitcast(I32),
+                    in_=Wo_scales.bitcast(I32)[:, r : 16 : 4, :].rearrange("g q n -> q g n"),
+                )
+
         def load_rows(rows, first, vector):
             nc.sync.dma_start(
                 out=rows[first : first + CHUNKS, :], in_=vector.rearrange("(c n) -> c n", c=CHUNKS)
             )
 
-        load_ctx(0)
+        load_ctx_pair(0, HEADS)
         load_rows(bias_rows, 0, bo)
-        for r in range(4):
-            nc.sync.dma_start(
-                out=w_scales[r : P : 32].bitcast(I32),
-                in_=Wo_scales.bitcast(I32)[:, r : 16 : 4, :].rearrange("g q n -> q g n"),
-            )
+        load_weight_scales()
         load_weight_chunk(0)
         load_features(0)
-        for c in range(1, CHUNKS):
-            load_weight_chunk(c)
+        load_weight_chunk(1)
+        load_features(1)
+        load_weight_chunk(2)
         load_rows(affine_rows, 0, ln_g)
         load_rows(affine_rows, CHUNKS, ln_b)
-        load_features(1)
-        load_ctx(1)
-        for b in range(2, BATCH):
-            load_ctx(b)
-            load_features(b)
+        load_ctx(2, 8)
+        load_features(2)
+        load_ctx(3, 8)
+        load_features(3)
+        for cols in (slice(WIDE, FEAT), slice(0, CHUNK)):
+            nc.sync.dma_start(out=shift_sb[:, cols], in_=ln_b[cols].partition_broadcast(P))
 
-        def spread(rows, row, dest):
+        def chunk(c):
+            return slice(CHUNK * c, CHUNK * (c + 1))
+
+        def select_row(rows, row, dest, stop):
             nc.tensor.matmul(
                 out=dest,
                 lhsT=ident_bf16[:, row : row + 1].to_broadcast([P, P]),
                 rhs=rows[:],
                 start=True,
-                stop=True,
+                stop=stop,
             )
 
-        def spread_bias():
-            for c in range(CHUNKS):
-                bias_bank = acc_banks.tile([P, CHUNK], F32, name="bias_bank", tag="acc")
-                spread(bias_rows, c, bias_bank[:])
-                nc.scalar.copy(out=bias_all[:, CHUNK * c : CHUNK * (c + 1)], in_=bias_bank[:])
+        def spread_bias(copy, c):
+            bank = acc_banks.tile([P, CHUNK], F32, name="bias_bank", tag="acc")
+            select_row(bias_rows, c, bank[:], True)
+            copy(out=bias_all[:, chunk(c)], in_=bank[:])
 
-        def spread_gain():
-            spread(affine_rows, 0, gain_lo[:, :CHUNK])
-            spread(affine_rows, 1, gain_lo[:, CHUNK:])
-            spread(affine_rows, 2, gain_hi)
-
-        def spread_shift():
-            spread(affine_rows, CHUNKS + 2, shift_hi)
-            spread(affine_rows, CHUNKS, shift_lo[:, :CHUNK])
-            spread(affine_rows, CHUNKS + 1, shift_lo[:, CHUNK:])
-
-        def shift_in_psum(cols):
+        def gain_in_psum(cols):
             if cols.start >= WIDE:
-                return shift_hi[:, cols.start - WIDE : cols.stop - WIDE]
-            return shift_lo[:, cols]
+                return gain_hi[:, cols.start - WIDE : cols.stop - WIDE]
+            return gain_lo[:, cols]
 
-        def shift_to_sbuf(c):
-            cols = slice(CHUNK * c, CHUNK * (c + 1))
-            nc.scalar.copy(out=shift_sb[:, cols], in_=shift_in_psum(cols))
+        def spread_gain(c):
+            select_row(affine_rows, c, gain_in_psum(chunk(c)), True)
 
-        def quantise(b):
+        def spread_shift(c, dest):
+            select_row(affine_rows, CHUNKS + c, dest, True)
+
+        def turn(b, first, count):
             words = x_sb[b][:].rearrange("s h d -> s (h d)").bitcast(F32)
-            grouped_words = grouped[b][:].bitcast(F32)
-            for first, count in ((0, 2), (2, 1)):
-                flipped = acc_banks.tile([P, 2 * count, P], F32, name="flipped", tag="acc")
-                for j in range(count):
-                    g = first + j
-                    for u in range(2):
-                        nc.tensor.transpose(
-                            flipped[:, 2 * j + u, :],
-                            words[:, 2 * P * g + u : 2 * P * (g + 1) : 2],
-                            ident_f32[:],
-                        )
-                nc.scalar.copy(
-                    out=grouped_words[:, 2 * P * first : 2 * P * (first + count)].rearrange(
-                        "p (j s u) -> p j s u", j=count, u=2
-                    ),
-                    in_=flipped[:].rearrange("p (j u) s -> p j s u", u=2),
-                )
-                nc.vector.quantize_mx(
-                    out=x_codes[b][:, P * first : P * (first + count)].bitcast(FP8X4),
-                    scales=x_scales[b][:, P * first : P * (first + count)],
-                    in_=grouped[b][:, K_PASS * first : K_PASS * (first + count)],
-                )
-
-        def residual(engine, b):
-            for c in range(CHUNKS):
-                cols = slice(CHUNK * c, CHUNK * (c + 1))
-                engine.tensor_tensor(
-                    out=resid[b][:, cols], in0=feat[b][:, cols], in1=bias_all[:, cols], op=ALU.add
-                )
-
-        def project(b):
-            for c in range(CHUNKS):
-                cols = slice(CHUNK * c, CHUNK * (c + 1))
-                acc = acc_banks.tile([P, CHUNK], F32, name="acc", tag="acc")
-                for g in range(PASSES):
-                    nc.tensor.matmul_mx(
-                        out=acc[:],
-                        lhsT=x_codes[b][:, P * g : P * (g + 1)].bitcast(FP8X4),
-                        lhsT_scale=x_scales[b][:, P * g : P * (g + 1)],
-                        rhs=w_words[:, c, g, :].bitcast(FP4X4),
-                        rhs_scale=w_scales[:, g, cols],
-                        start=(g == 0),
-                        stop=(g == PASSES - 1),
+            flipped = acc_banks.tile([P, 2 * count, P], F32, name="flipped", tag="acc")
+            for j in range(count):
+                g = first + j
+                for u in range(2):
+                    nc.tensor.transpose(
+                        flipped[:, 2 * j + u, :],
+                        words[:, 2 * P * g + u : 2 * P * (g + 1) : 2],
+                        ident_f32[:],
                     )
-                nc.vector.scalar_tensor_tensor(
-                    out=y[b][:, cols],
-                    in0=resid[b][:, cols],
-                    scalar=1.0,
-                    in1=acc[:],
-                    op0=ALU.mult,
-                    op1=ALU.add,
-                    accum_out=chunk_sums[b][:, c : c + 1],
+            return flipped
+
+        def group(copy, b, first, count, flipped):
+            grouped_words = grouped[b][:].bitcast(F32)
+            copy(
+                out=grouped_words[:, 2 * P * first : 2 * P * (first + count)].rearrange(
+                    "p (j s u) -> p j s u", j=count, u=2
+                ),
+                in_=flipped[:].rearrange("p (j u) s -> p j s u", u=2),
+            )
+
+        def quant(b, first, count):
+            nc.vector.quantize_mx(
+                out=x_codes[b][:, P * first : P * (first + count)].bitcast(FP8X4),
+                scales=x_scales[b][:, P * first : P * (first + count)],
+                in_=grouped[b][:, K_PASS * first : K_PASS * (first + count)],
+            )
+
+        def residual(engine, b, c):
+            engine.tensor_tensor(
+                out=resid[b][:, chunk(c)],
+                in0=feat[b][:, chunk(c)],
+                in1=bias_all[:, chunk(c)],
+                op=ALU.add,
+            )
+
+        def residual_by_matmul(b, c):
+            bank = acc_banks.tile([P, CHUNK], F32, name="resid_bank", tag="acc")
+            select_row(bias_rows, c, bank[:], False)
+            nc.tensor.matmul(
+                out=bank[:], lhsT=ident_bf16[:], rhs=feat[b][:, chunk(c)], start=False, stop=True
+            )
+            nc.scalar.copy(out=resid[b][:, chunk(c)], in_=bank[:])
+
+        def project(b, c):
+            acc = acc_banks.tile([P, CHUNK], F32, name="acc", tag="acc")
+            for g in range(PASSES):
+                nc.tensor.matmul_mx(
+                    out=acc[:],
+                    lhsT=x_codes[b][:, P * g : P * (g + 1)].bitcast(FP8X4),
+                    lhsT_scale=x_scales[b][:, P * g : P * (g + 1)],
+                    rhs=w_words[:, c, g, :].bitcast(FP4X4),
+                    rhs_scale=w_scales[:, g, chunk(c)],
+                    start=(g == 0),
+                    stop=(g == PASSES - 1),
                 )
+            nc.vector.scalar_tensor_tensor(
+                out=y[b][:, chunk(c)],
+                in0=resid[b][:, chunk(c)],
+                scalar=1.0,
+                in1=acc[:],
+                op0=ALU.mult,
+                op1=ALU.add,
+                accum_out=chunk_sums[b][:, c : c + 1],
+            )
+
+        def mean(b):
             nc.scalar.activation(
                 out=chunk_means[b][:], in_=chunk_sums[b][:], func=ACT.Copy, scale=-1.0 / FEAT,
                 accum_out=neg_mean[b][:],
@@ -237,83 +273,205 @@ def tile_hierarchicalattention_pb_kernel(
                 scale=1.0 / FEAT,
             )
 
-        def gain_cols(b, cols, gain):
+        def provisional_mean(b):
+            nc.scalar.activation(
+                out=first_mean[b][:], in_=chunk_sums[b][:, 0:1], func=ACT.Copy, scale=-1.0 / CHUNK
+            )
+
+        def chunk_square(b, c):
+            squares = scratch.tile([P, CHUNK], F32, name="chunk_squares")
+            nc.scalar.activation(
+                out=squares[:], in_=y[b][:, chunk(c)], func=ACT.Square, bias=first_mean[b][:],
+                scale=1.0, accum_out=chunk_sq[b][:, c : c + 1],
+            )
+
+        def combine_variance(b):
+            nc.scalar.activation(
+                out=mean_gap[b][:], in_=neg_mean[b][:], func=ACT.Square, bias=first_mean[b][:],
+                scale=-1.0,
+            )
+            nc.scalar.activation(
+                out=chunk_vars[b][:], in_=chunk_sq[b][:], func=ACT.Copy, scale=1.0 / FEAT,
+                accum_out=sum_sq[b][:],
+            )
+            nc.scalar.activation(
+                out=eps_gap[b][:], in_=mean_gap[b][:], func=ACT.Copy, scale=-1.0, bias=LN_EPS
+            )
+            nc.scalar.activation(
+                out=rstd[b][:], in_=sum_sq[b][:], func=ACT.Abs_reciprocal_sqrt, bias=eps_gap[b][:],
+                scale=1.0,
+            )
+
+        def gain(b, first, stop):
+            cols = slice(first, stop)
             nc.vector.scalar_tensor_tensor(
                 out=gained[b][:, cols],
                 in0=y[b][:, cols],
                 scalar=neg_mean[b][:],
-                in1=gain,
+                in1=gain_in_psum(cols),
                 op0=ALU.add,
                 op1=ALU.mult,
             )
 
-        def centre_and_gain(b):
-            gain_cols(b, slice(WIDE, FEAT), gain_hi)
-            gain_cols(b, slice(0, WIDE), gain_lo[:])
-
-        def shift_wide(b, step):
-            last = FEAT - NARROW[b]
-            for first in range(0, last, step):
-                cols = slice(first, min(first + step, last))
-                nc.vector.scalar_tensor_tensor(
-                    out=result[b][:, cols],
-                    in0=gained[b][:, cols],
-                    scalar=rstd[b][:],
-                    in1=shift_in_psum(cols),
-                    op0=ALU.mult,
-                    op1=ALU.add,
-                )
-                nc.sync.dma_start(out=out[b, :, cols], in_=result[b][:, cols])
-
-        def shift_narrow(b):
-            for stop in range(FEAT, FEAT - NARROW[b], -CHUNK):
-                cols = slice(max(stop - CHUNK, FEAT - NARROW[b]), stop)
-                nc.scalar.activation(
-                    out=scaled[b][:, cols], in_=gained[b][:, cols], func=ACT.Copy, scale=rstd[b][:]
-                )
-                nc.gpsimd.tensor_tensor(
-                    out=result[b][:, cols], in0=scaled[b][:, cols], in1=shift_sb[:, cols], op=ALU.add
-                )
-
-        def store_narrow(b):
-            for stop in range(FEAT, FEAT - NARROW[b], -CHUNK):
-                cols = slice(max(stop - CHUNK, FEAT - NARROW[b]), stop)
-                nc.sync.dma_start(out=out[b, :, cols], in_=result[b][:, cols])
-
-        quantise(0)
-        spread_bias()
-        residual(nc.vector, 0)
-        for b in range(1, BATCH):
-            residual(nc.gpsimd, b)
-        for b in range(BATCH):
-            if b == 1:
-                shift_to_sbuf(2)
-            if b == 2:
-                shift_to_sbuf(1)
-            if b > 0:
-                shift_narrow(b - 1)
-            project(b)
-            if b == 0:
-                spread_gain()
-            if b > 0:
-                shift_wide(b - 1, WIDE)
-            if b > 1:
-                store_narrow(b - 2)
-            if b == 1:
-                quantise(2)
-            if b == 0:
-                gain_cols(b, slice(WIDE, FEAT), gain_hi)
-                gain_cols(b, slice(0, CHUNK), gain_lo[:, :CHUNK])
-                quantise(1)
-                gain_cols(b, slice(CHUNK, WIDE), gain_lo[:, CHUNK:])
+        def store(t, cols):
+            if t < 2:
+                for b in range(2):
+                    nc.sync.dma_start(
+                        out=out[b].rearrange("(i e) n -> e i n", e=2)[t][:, cols],
+                        in_=result[t][b : P : 2, cols],
+                    )
             else:
-                centre_and_gain(b)
-            if b == 1:
-                quantise(3)
-            if b == 0:
-                spread_shift()
-            variance(b)
-        shift_narrow(BATCH - 1)
-        store_narrow(BATCH - 2)
-        shift_wide(BATCH - 1, CHUNK)
-        store_narrow(BATCH - 1)
+                nc.sync.dma_start(out=out[t, :, cols], in_=result[t][:, cols])
+
+        def shift(b, first, stop, rows):
+            cols = slice(first, stop)
+            nc.vector.scalar_tensor_tensor(
+                out=result[b][:, cols],
+                in0=gained[b][:, cols],
+                scalar=rstd[b][:],
+                in1=rows[:, first % CHUNK : first % CHUNK + stop - first],
+                op0=ALU.mult,
+                op1=ALU.add,
+            )
+
+        def scale(b, first, stop):
+            cols = slice(first, stop)
+            nc.scalar.activation(
+                out=scaled[b][:, cols], in_=gained[b][:, cols], func=ACT.Copy, scale=rstd[b][:]
+            )
+
+        def add_shift(b, first, stop):
+            cols = slice(first, stop)
+            nc.gpsimd.tensor_tensor(
+                out=result[b][:, cols], in0=scaled[b][:, cols], in1=shift_sb[:, cols], op=ALU.add
+            )
+
+        def make_diag(b):
+            nc.scalar.activation(
+                out=rstd_diag[b][:], in_=ident_f32[:], func=ACT.Copy, scale=rstd[b][:]
+            )
+
+        def shift_by_matmul(b, c):
+            bank = acc_banks.tile([P, CHUNK], F32, name="shift_bank", tag="acc")
+            select_row(affine_rows, CHUNKS + c, bank[:], False)
+            nc.tensor.matmul(
+                out=bank[:], lhsT=rstd_diag[b][:], rhs=gained[b][:, chunk(c)], start=False, stop=True
+            )
+            nc.scalar.copy(out=result[b][:, chunk(c)], in_=bank[:])
+
+        def shift_bank(c):
+            bank = acc_banks.tile([P, CHUNK], F32, name="shift_rows", tag="acc")
+            spread_shift(c, bank[:])
+            return bank
+
+        V, S, G = nc.vector, nc.scalar, nc.gpsimd
+        split_pair(V.tensor_copy, 0, 0, 8)
+        split_pair(V.tensor_copy, 0, 8, 12)
+        split_pair(V.tensor_copy, 1, 0, 12)
+        spread_bias(V.tensor_copy, 0)
+        spread_bias(V.tensor_copy, 1)
+        f = turn(0, 0, 2)
+        group(S.copy, 0, 0, 2, f)
+        f = turn(0, 2, 1)
+        group(S.copy, 0, 2, 1, f)
+        quant(0, 0, 2)
+        quant(0, 2, 1)
+        f = turn(1, 0, 2)
+        group(S.copy, 1, 0, 2, f)
+        f2 = turn(1, 2, 1)
+        group(S.copy, 1, 2, 1, f2)
+        spread_bias(S.copy, 2)
+        residual(V, 0, 0)
+        residual(G, 0, 1)
+        quant(1, 0, 2)
+        quant(1, 2, 1)
+        project(0, 0)
+        residual(G, 0, 2)
+        provisional_mean(0)
+        chunk_square(0, 0)
+        residual(V, 1, 0)
+        project(0, 1)
+        chunk_square(0, 1)
+        project(1, 0)
+        residual(G, 1, 1)
+        residual(G, 1, 2)
+        project(0, 2)
+        mean(0)
+        chunk_square(0, 2)
+        combine_variance(0)
+        make_diag(0)
+        project(1, 1)
+        spread_gain(0)
+        spread_gain(1)
+        gain(0, 0, CHUNK)
+        project(1, 2)
+        mean(1)
+        spread_gain(2)
+        spread_shift(0, shift_first)
+        f = turn(2, 0, 2)
+        group(S.copy, 2, 0, 2, f)
+        f = turn(2, 2, 1)
+        group(S.copy, 2, 2, 1, f)
+        gain(0, CHUNK, WIDE)
+        for c in range(CHUNKS):
+            residual(G, 2, c)
+        gain(0, WIDE, FEAT)
+        scale(0, WIDE, FEAT)
+        shift(0, 0, CHUNK, shift_first)
+        store(0, chunk(0))
+        quant(2, 0, 2)
+        quant(2, 2, 1)
+        f = turn(3, 0, 2)
+        f2 = turn(3, 2, 1)
+        group(S.copy, 3, 0, 2, f)
+        group(S.copy, 3, 2, 1, f2)
+        variance(1)
+        make_diag(1)
+        shift_by_matmul(0, 1)
+        store(0, chunk(1))
+        gain(1, 0, WIDE)
+        gain(1, WIDE, FEAT)
+        add_shift(0, WIDE, FEAT)
+        store(0, chunk(2))
+        for c in range(CHUNKS):
+            residual(G, 3, c)
+        for c in range(CHUNKS):
+            project(2, c)
+        scale(1, WIDE, FEAT)
+        mean(2)
+        quant(3, 0, 2)
+        quant(3, 2, 1)
+        variance(2)
+        make_diag(2)
+        gain(2, 0, WIDE)
+        gain(2, WIDE, FEAT)
+        scale(2, WIDE, FEAT)
+        scale(1, 0, CHUNK)
+        shift_by_matmul(1, 1)
+        add_shift(1, WIDE, FEAT)
+        store(1, chunk(2))
+        store(1, chunk(1))
+        for c in range(CHUNKS):
+            project(3, c)
+        mean(3)
+        variance(3)
+        add_shift(2, WIDE, FEAT)
+        add_shift(1, 0, CHUNK)
+        shift(2, 0, CHUNK, shift_first)
+        store(2, chunk(0))
+        store(2, chunk(2))
+        store(1, chunk(0))
+        gain(3, WIDE, FEAT)
+        gain(3, 0, WIDE)
+        shift_mid = shift_bank(1)
+        for first, stop in ((1280, 1536), (1024, 1280)):
+            scale(3, first, stop)
+            add_shift(3, first, stop)
+        shift_by_matmul(2, 1)
+        shift(3, 0, 512, shift_first)
+        store(3, slice(0, 512))
+        store(3, slice(1280, 1536))
+        store(2, chunk(1))
+        shift(3, 512, 1024, shift_mid)
+        store(3, slice(512, 1024))
+        store(3, slice(1024, 1280))

@@ -431,10 +431,10 @@ def tile_hierarchicalattention_pb_kernel(
         store(0, chunk(1))
         gain(1, 0, WIDE)
         gain(1, WIDE, FEAT)
-        add_shift(0, WIDE, FEAT)
-        store(0, chunk(2))
         for c in range(CHUNKS):
             residual(G, 3, c)
+        add_shift(0, WIDE, FEAT)
+        store(0, chunk(2))
         for c in range(CHUNKS):
             project(2, c)
         scale(1, WIDE, FEAT)

@@ -145,9 +145,9 @@ def tile_hierarchicalattention_pb_kernel(
             )
 
         load_ctx_pair(0, HEADS)
+        load_weight_chunk(0)
         load_rows(bias_rows, 0, bo)
         load_weight_scales()
-        load_weight_chunk(0)
         load_features(0)
         load_weight_chunk(1)
         load_features(1)

@@ -145,8 +145,8 @@ def tile_hierarchicalattention_pb_kernel(
             )
 
         load_ctx_pair(0, HEADS)
-        load_weight_chunk(0)
         load_rows(bias_rows, 0, bo)
+        load_weight_chunk(0)
         load_weight_scales()
         load_features(0)
         load_weight_chunk(1)
@@ -439,16 +439,17 @@ def tile_hierarchicalattention_pb_kernel(
             project(2, c)
         scale(1, WIDE, FEAT)
         mean(2)
+        scale(1, 0, CHUNK)
         quant(3, 0, 2)
         quant(3, 2, 1)
         variance(2)
         make_diag(2)
         gain(2, 0, WIDE)
         gain(2, WIDE, FEAT)
-        scale(2, WIDE, FEAT)
-        scale(1, 0, CHUNK)
         shift_by_matmul(1, 1)
+        scale(2, WIDE, FEAT)
         add_shift(1, WIDE, FEAT)
+        add_shift(1, 0, CHUNK)
         store(1, chunk(2))
         store(1, chunk(1))
         for c in range(CHUNKS):
@@ -456,22 +457,23 @@ def tile_hierarchicalattention_pb_kernel(
         mean(3)
         variance(3)
         add_shift(2, WIDE, FEAT)
-        add_shift(1, 0, CHUNK)
         shift(2, 0, CHUNK, shift_first)
         store(2, chunk(0))
-        store(2, chunk(2))
         store(1, chunk(0))
+        store(2, chunk(2))
         gain(3, WIDE, FEAT)
         gain(3, 0, WIDE)
         shift_mid = shift_bank(1)
-        for first, stop in ((1280, 1536), (1024, 1280)):
-            scale(3, first, stop)
-            add_shift(3, first, stop)
+        scale(3, 1280, 1536)
+        add_shift(3, 1280, 1536)
         shift_by_matmul(2, 1)
-        shift(3, 0, 512, shift_first)
-        store(3, slice(0, 512))
-        store(3, slice(1280, 1536))
+        shift(3, 0, 256, shift_first)
+        store(3, slice(0, 256))
+        shift(3, 256, 512, shift_first)
+        store(3, slice(256, 512))
         store(2, chunk(1))
         shift(3, 512, 1024, shift_mid)
         store(3, slice(512, 1024))
+        store(3, slice(1280, 1536))
+        shift(3, 1024, 1280, shift_sb[:, WIDE:FEAT])
         store(3, slice(1024, 1280))

from contextlib import ExitStack

import concourse.mybir as mybir
from concourse.masks import make_identity

F32 = mybir.dt.float32
BF16 = mybir.dt.bfloat16
I32 = mybir.dt.int32
U32 = mybir.dt.uint32
U8 = mybir.dt.uint8
FP8X4 = mybir.dt.float8_e4m3fn_x4
FP4X4 = mybir.dt.float4_e2m1fn_x4
ALU = mybir.AluOpType
ACT = mybir.ActivationFunctionType

P = 128
PACK = 4
K_PASS = P * PACK
BATCH = 4
HEADS = 12
HEAD_DIM = 128
FEAT = 1536
PASSES = FEAT // K_PASS
HEADS_PER_PASS = K_PASS // HEAD_DIM
CHUNK = 512
CHUNKS = FEAT // CHUNK
WIDE = 2 * CHUNK
LN_EPS = 1e-5

FLOPS = 2 * BATCH * P * FEAT * FEAT


def tile_hierarchicalattention_pb_kernel(
    tc, ctx_heads, Wo_words, Wo_scales, bo, features, ln_g, ln_b, out
):
    nc = tc.nc
    with ExitStack() as stack:
        keep = stack.enter_context(tc.tile_pool(name="keep", bufs=1))
        scratch = stack.enter_context(tc.tile_pool(name="scratch", bufs=2))
        gain_banks = stack.enter_context(tc.psum_pool(name="gain_banks", bufs=1))
        acc_banks = stack.enter_context(tc.psum_pool(name="acc_banks", bufs=6))
        stack.enter_context(tc.manual_schedule())

        x_pair = keep.tile([P, HEADS, 2, HEAD_DIM], BF16, name="x_pair")
        x_sb = [keep.tile([P, HEADS, HEAD_DIM], BF16, name="x%d" % b) for b in range(BATCH)]
        feat = [keep.tile([P, FEAT], BF16, name="feat%d" % b) for b in range(BATCH)]
        grouped = [
            keep.tile([P, PASSES * P * PACK], BF16, name="grouped%d" % b, align_bytes=64)
            for b in range(BATCH)
        ]
        x_codes = [
            keep.tile([P, PASSES * P], U32, name="x_codes%d" % b, align_bytes=64)
            for b in range(BATCH)
        ]
        x_scales = [
            keep.tile([P, PASSES * P], U8, name="x_scales%d" % b, align_bytes=64)
            for b in range(BATCH)
        ]
        w_words = keep.tile([P, CHUNKS, PASSES, 2 * CHUNK], U8, name="w_words", align_bytes=64)
        w_scales = keep.tile([P, PASSES, FEAT], U8, name="w_scales", align_bytes=64)
        resid = [keep.tile([P, FEAT], F32, name="resid%d" % b) for b in range(BATCH)]
        y = [keep.tile([P, FEAT], F32, name="y%d" % b) for b in range(BATCH)]
        gained = [keep.tile([P, FEAT], F32, name="gained%d" % b) for b in range(BATCH)]
        result = [keep.tile([P, FEAT], F32, name="result%d" % b) for b in range(BATCH)]
        chunk_sums = [keep.tile([P, CHUNKS], F32, name="chunk_sums%d" % b) for b in range(BATCH)]
        chunk_means = [keep.tile([P, CHUNKS], F32, name="chunk_means%d" % b) for b in range(BATCH)]
        neg_mean = [keep.tile([P, 1], F32, name="neg_mean%d" % b) for b in range(BATCH)]
        sum_sq = [keep.tile([P, 1], F32, name="sum_sq%d" % b) for b in range(BATCH)]
        first_mean = [keep.tile([P, 1], F32, name="first_mean%d" % b) for b in range(BATCH)]
        chunk_sq = [keep.tile([P, CHUNKS], F32, name="chunk_sq%d" % b) for b in range(BATCH)]
        chunk_vars = [keep.tile([P, CHUNKS], F32, name="chunk_vars%d" % b) for b in range(BATCH)]
        mean_gap = [keep.tile([P, 1], F32, name="mean_gap%d" % b) for b in range(BATCH)]
        eps_gap = [keep.tile([P, 1], F32, name="eps_gap%d" % b) for b in range(BATCH)]
        rstd = [keep.tile([P, 1], F32, name="rstd%d" % b) for b in range(BATCH)]
        ident_f32 = keep.tile([P, P], F32, name="ident_f32")
        ident_bf16 = keep.tile([P, P], BF16, name="ident_bf16")
        bias_rows = keep.tile([P, CHUNK], BF16, name="bias_rows")
        affine_rows = keep.tile([P, CHUNK], BF16, name="affine_rows")
        bias_all = keep.tile([P, FEAT], BF16, name="bias_all")
        eps = keep.tile([P, 1], F32, name="eps")
        warm = keep.tile([P, 1], F32, name="warm")
        gain_lo = gain_banks.tile([P, WIDE], BF16, name="gain_lo")
        both_hi = gain_banks.tile([P, 2 * (FEAT - WIDE)], BF16, name="both_hi")
        gain_hi = both_hi[:, : FEAT - WIDE]
        shift_first = both_hi[:, FEAT - WIDE :]
        shift_sb = keep.tile([P, FEAT], BF16, name="shift_sb")
        scaled = [keep.tile([P, FEAT], F32, name="scaled%d" % b) for b in range(BATCH)]
        rstd_diag = [keep.tile([P, P], F32, name="rstd_diag%d" % b) for b in range(BATCH)]

        nc.vector.memset(bias_rows[:], 0.0)
        nc.vector.memset(w_scales[:].bitcast(I32), 0)
        nc.vector.memset(affine_rows[:], 0.0)
        nc.vector.memset(eps[:], LN_EPS)
        make_identity(nc, ident_bf16[:])
        make_identity(nc, ident_f32[:])
        nc.scalar.activation(out=warm[:], in_=eps[:], func=ACT.Abs_reciprocal_sqrt)

        def load_ctx_pair(first, stop):
            heads = slice(first, stop)
            for b in range(2):
                nc.sync.dma_start(
                    out=x_pair[b : P : 2, heads],
                    in_=ctx_heads[b, heads].rearrange("h (i e) d -> i h e d", e=2),
                )

        def split_pair(copy, e, first, stop):
            heads = slice(first, stop)
            copy(out=x_sb[e][:, heads, :], in_=x_pair[:, heads, e, :])

        def load_ctx(b, *bounds):
            for first, stop in zip((0,) + bounds, bounds + (HEADS,)):
                heads = slice(first, stop)
                nc.sync.dma_start(
                    out=x_sb[b][:, heads, :], in_=ctx_heads[b, heads].rearrange("h s d -> s h d")
                )

        def load_features(t):
            if t < 2:
                for b in range(2):
                    nc.sync.dma_start(
                        out=feat[t][b : P : 2, :],
                        in_=features[b].rearrange("(i e) n -> e i n", e=2)[t],
                    )
            else:
                nc.sync.dma_start(out=feat[t][:], in_=features[t])

        def load_weight_chunk(c):
            nc.sync.dma_start(
                out=w_words[:, c].bitcast(I32),
                in_=Wo_words.bitcast(I32)[:, :, (CHUNK // 2) * c : (CHUNK // 2) * (c + 1)].rearrange(
                    "g p n -> p g n"
                ),
            )

        def load_weight_scales():
            for r in range(4):
                nc.sync.dma_start(
                    out=w_scales[r : P : 32].bitcast(I32),
                    in_=Wo_scales.bitcast(I32)[:, r : 16 : 4, :].rearrange("g q n -> q g n"),
                )

        def load_rows(rows, first, vector):
            nc.sync.dma_start(
                out=rows[first : first + CHUNKS, :], in_=vector.rearrange("(c n) -> c n", c=CHUNKS)
            )

        load_ctx_pair(0, HEADS)
        load_rows(bias_rows, 0, bo)
        load_weight_chunk(0)
        load_weight_scales()
        load_features(0)
        load_weight_chunk(1)
        load_features(1)
        load_weight_chunk(2)
        load_rows(affine_rows, 0, ln_g)
        load_rows(affine_rows, CHUNKS, ln_b)
        load_ctx(2, 8)
        load_features(2)
        load_ctx(3, 8)
        load_features(3)
        for cols in (slice(WIDE, FEAT), slice(0, CHUNK)):
            nc.sync.dma_start(out=shift_sb[:, cols], in_=ln_b[cols].partition_broadcast(P))

        def chunk(c):
            return slice(CHUNK * c, CHUNK * (c + 1))

        def select_row(rows, row, dest, stop):
            nc.tensor.matmul(
                out=dest,
                lhsT=ident_bf16[:, row : row + 1].to_broadcast([P, P]),
                rhs=rows[:],
                start=True,
                stop=stop,
            )

        def spread_bias(copy, c):
            bank = acc_banks.tile([P, CHUNK], F32, name="bias_bank", tag="acc")
            select_row(bias_rows, c, bank[:], True)
            copy(out=bias_all[:, chunk(c)], in_=bank[:])

        def gain_in_psum(cols):
            if cols.start >= WIDE:
                return gain_hi[:, cols.start - WIDE : cols.stop - WIDE]
            return gain_lo[:, cols]

        def spread_gain(c):
            select_row(affine_rows, c, gain_in_psum(chunk(c)), True)

        def spread_shift(c, dest):
            select_row(affine_rows, CHUNKS + c, dest, True)

        def turn(b, first, count):
            words = x_sb[b][:].rearrange("s h d -> s (h d)").bitcast(F32)
            flipped = acc_banks.tile([P, 2 * count, P], F32, name="flipped", tag="acc")
            for j in range(count):
                g = first + j
                for u in range(2):
                    nc.tensor.transpose(
                        flipped[:, 2 * j + u, :],
                        words[:, 2 * P * g + u : 2 * P * (g + 1) : 2],
                        ident_f32[:],
                    )
            return flipped

        def group(copy, b, first, count, flipped):
            grouped_words = grouped[b][:].bitcast(F32)
            copy(
                out=grouped_words[:, 2 * P * first : 2 * P * (first + count)].rearrange(
                    "p (j s u) -> p j s u", j=count, u=2
                ),
                in_=flipped[:].rearrange("p (j u) s -> p j s u", u=2),
            )

        def quant(b, first, count):
            nc.vector.quantize_mx(
                out=x_codes[b][:, P * first : P * (first + count)].bitcast(FP8X4),
                scales=x_scales[b][:, P * first : P * (first + count)],
                in_=grouped[b][:, K_PASS * first : K_PASS * (first + count)],
            )

        def residual(engine, b, c):
            engine.tensor_tensor(
                out=resid[b][:, chunk(c)],
                in0=feat[b][:, chunk(c)],
                in1=bias_all[:, chunk(c)],
                op=ALU.add,
            )

        def residual_by_matmul(b, c):
            bank = acc_banks.tile([P, CHUNK], F32, name="resid_bank", tag="acc")
            select_row(bias_rows, c, bank[:], False)
            nc.tensor.matmul(
                out=bank[:], lhsT=ident_bf16[:], rhs=feat[b][:, chunk(c)], start=False, stop=True
            )
            nc.scalar.copy(out=resid[b][:, chunk(c)], in_=bank[:])

        def project(b, c):
            acc = acc_banks.tile([P, CHUNK], F32, name="acc", tag="acc")
            for g in range(PASSES):
                nc.tensor.matmul_mx(
                    out=acc[:],
                    lhsT=x_codes[b][:, P * g : P * (g + 1)].bitcast(FP8X4),
                    lhsT_scale=x_scales[b][:, P * g : P * (g + 1)],
                    rhs=w_words[:, c, g, :].bitcast(FP4X4),
                    rhs_scale=w_scales[:, g, chunk(c)],
                    start=(g == 0),
                    stop=(g == PASSES - 1),
                )
            nc.vector.scalar_tensor_tensor(
                out=y[b][:, chunk(c)],
                in0=resid[b][:, chunk(c)],
                scalar=1.0,
                in1=acc[:],
                op0=ALU.mult,
                op1=ALU.add,
                accum_out=chunk_sums[b][:, c : c + 1],
            )

        def mean(b):
            nc.scalar.activation(
                out=chunk_means[b][:], in_=chunk_sums[b][:], func=ACT.Copy, scale=-1.0 / FEAT,
                accum_out=neg_mean[b][:],
            )

        def variance(b):
            squares = scratch.tile([P, FEAT], F32, name="squares")
            nc.scalar.activation(
                out=squares[:], in_=y[b][:], func=ACT.Square, bias=neg_mean[b][:], scale=1.0,
                accum_out=sum_sq[b][:],
            )
            nc.scalar.activation(
                out=rstd[b][:], in_=sum_sq[b][:], func=ACT.Abs_reciprocal_sqrt, bias=eps[:],
                scale=1.0 / FEAT,
            )

        def provisional_mean(b):
            nc.scalar.activation(
                out=first_mean[b][:], in_=chunk_sums[b][:, 0:1], func=ACT.Copy, scale=-1.0 / CHUNK
            )

        def chunk_square(b, c):
            squares = scratch.tile([P, CHUNK], F32, name="chunk_squares")
            nc.scalar.activation(
                out=squares[:], in_=y[b][:, chunk(c)], func=ACT.Square, bias=first_mean[b][:],
                scale=1.0, accum_out=chunk_sq[b][:, c : c + 1],
            )

        def combine_variance(b):
            nc.scalar.activation(
                out=mean_gap[b][:], in_=neg_mean[b][:], func=ACT.Square, bias=first_mean[b][:],
                scale=-1.0,
            )
            nc.scalar.activation(
                out=chunk_vars[b][:], in_=chunk_sq[b][:], func=ACT.Copy, scale=1.0 / FEAT,
                accum_out=sum_sq[b][:],
            )
            nc.scalar.activation(
                out=eps_gap[b][:], in_=mean_gap[b][:], func=ACT.Copy, scale=-1.0, bias=LN_EPS
            )
            nc.scalar.activation(
                out=rstd[b][:], in_=sum_sq[b][:], func=ACT.Abs_reciprocal_sqrt, bias=eps_gap[b][:],
                scale=1.0,
            )

        def gain(b, first, stop):
            cols = slice(first, stop)
            nc.vector.scalar_tensor_tensor(
                out=gained[b][:, cols],
                in0=y[b][:, cols],
                scalar=neg_mean[b][:],
                in1=gain_in_psum(cols),
                op0=ALU.add,
                op1=ALU.mult,
            )

        def store(t, cols):
            if t < 2:
                for b in range(2):
                    nc.sync.dma_start(
                        out=out[b].rearrange("(i e) n -> e i n", e=2)[t][:, cols],
                        in_=result[t][b : P : 2, cols],
                    )
            else:
                nc.sync.dma_start(out=out[t, :, cols], in_=result[t][:, cols])

        def shift(b, first, stop, rows):
            cols = slice(first, stop)
            nc.vector.scalar_tensor_tensor(
                out=result[b][:, cols],
                in0=gained[b][:, cols],
                scalar=rstd[b][:],
                in1=rows[:, first % CHUNK : first % CHUNK + stop - first],
                op0=ALU.mult,
                op1=ALU.add,
            )

        def scale(b, first, stop):
            cols = slice(first, stop)
            nc.scalar.activation(
                out=scaled[b][:, cols], in_=gained[b][:, cols], func=ACT.Copy, scale=rstd[b][:]
            )

        def add_shift(b, first, stop):
            cols = slice(first, stop)
            nc.gpsimd.tensor_tensor(
                out=result[b][:, cols], in0=scaled[b][:, cols], in1=shift_sb[:, cols], op=ALU.add
            )

        def make_diag(b):
            nc.scalar.activation(
                out=rstd_diag[b][:], in_=ident_f32[:], func=ACT.Copy, scale=rstd[b][:]
            )

        def shift_by_matmul(b, c):
            bank = acc_banks.tile([P, CHUNK], F32, name="shift_bank", tag="acc")
            select_row(affine_rows, CHUNKS + c, bank[:], False)
            nc.tensor.matmul(
                out=bank[:], lhsT=rstd_diag[b][:], rhs=gained[b][:, chunk(c)], start=False, stop=True
            )
            nc.scalar.copy(out=result[b][:, chunk(c)], in_=bank[:])

        def shift_bank(c):
            bank = acc_banks.tile([P, CHUNK], F32, name="shift_rows", tag="acc")
            spread_shift(c, bank[:])
            return bank

        V, S, G = nc.vector, nc.scalar, nc.gpsimd
        split_pair(V.tensor_copy, 0, 0, 8)
        split_pair(V.tensor_copy, 0, 8, 12)
        split_pair(V.tensor_copy, 1, 0, 12)
        spread_bias(V.tensor_copy, 0)
        spread_bias(V.tensor_copy, 1)
        f = turn(0, 0, 2)
        group(S.copy, 0, 0, 2, f)
        f = turn(0, 2, 1)
        group(S.copy, 0, 2, 1, f)
        quant(0, 0, 2)
        quant(0, 2, 1)
        f = turn(1, 0, 2)
        group(S.copy, 1, 0, 2, f)
        f2 = turn(1, 2, 1)
        group(S.copy, 1, 2, 1, f2)
        spread_bias(S.copy, 2)
        residual(V, 0, 0)
        residual(G, 0, 1)
        quant(1, 0, 2)
        quant(1, 2, 1)
        project(0, 0)
        residual(G, 0, 2)
        provisional_mean(0)
        chunk_square(0, 0)
        residual(V, 1, 0)
        project(0, 1)
        chunk_square(0, 1)
        project(1, 0)
        residual(G, 1, 1)
        residual(G, 1, 2)
        project(0, 2)
        mean(0)
        chunk_square(0, 2)
        combine_variance(0)
        make_diag(0)
        project(1, 1)
        spread_gain(0)
        spread_gain(1)
        gain(0, 0, CHUNK)
        project(1, 2)
        mean(1)
        spread_gain(2)
        spread_shift(0, shift_first)
        f = turn(2, 0, 2)
        group(S.copy, 2, 0, 2, f)
        f = turn(2, 2, 1)
        group(S.copy, 2, 2, 1, f)
        gain(0, CHUNK, WIDE)
        for c in range(CHUNKS):
            residual(G, 2, c)
        gain(0, WIDE, FEAT)
        scale(0, WIDE, FEAT)
        shift(0, 0, CHUNK, shift_first)
        store(0, chunk(0))
        quant(2, 0, 2)
        quant(2, 2, 1)
        f = turn(3, 0, 2)
        f2 = turn(3, 2, 1)
        group(S.copy, 3, 0, 2, f)
        group(S.copy, 3, 2, 1, f2)
        variance(1)
        make_diag(1)
        shift_by_matmul(0, 1)
        store(0, chunk(1))
        gain(1, 0, WIDE)
        gain(1, WIDE, FEAT)
        for c in range(CHUNKS):
            residual(G, 3, c)
        add_shift(0, WIDE, FEAT)
        store(0, chunk(2))
        for c in range(CHUNKS):
            project(2, c)
        scale(1, WIDE, FEAT)
        mean(2)
        scale(1, 0, CHUNK)
        quant(3, 0, 2)
        quant(3, 2, 1)
        variance(2)
        make_diag(2)
        gain(2, 0, WIDE)
        gain(2, WIDE, FEAT)
        shift_by_matmul(1, 1)
        scale(2, WIDE, FEAT)
        add_shift(1, WIDE, FEAT)
        add_shift(1, 0, CHUNK)
        store(1, chunk(2))
        store(1, chunk(1))
        for c in range(CHUNKS):
            project(3, c)
        mean(3)
        variance(3)
        add_shift(2, WIDE, FEAT)
        shift(2, 0, CHUNK, shift_first)
        store(2, chunk(0))
        store(1, chunk(0))
        store(2, chunk(2))
        gain(3, WIDE, FEAT)
        gain(3, 0, WIDE)
        shift_mid = shift_bank(1)
        scale(3, 1280, 1536)
        add_shift(3, 1280, 1536)
        shift_by_matmul(2, 1)
        shift(3, 0, 256, shift_first)
        store(3, slice(0, 256))
        shift(3, 256, 512, shift_first)
        store(3, slice(256, 512))
        store(2, chunk(1))
        shift(3, 512, 1024, shift_mid)
        store(3, slice(512, 1024))
        store(3, slice(1280, 1536))
        shift(3, 1024, 1280, shift_sb[:, WIDE:FEAT])
        store(3, slice(1024, 1280))
